import numpy as np
import ml_dtypes


def mxq(x, axis, fmt="e4m3"):
    dtype, down = {"e4m3": (ml_dtypes.float8_e4m3fn, 7), "e5m2": (ml_dtypes.float8_e5m2, 14)}[fmt]
    v = np.moveaxis(np.asarray(x, np.float32).astype(ml_dtypes.bfloat16).astype(np.float64), axis, -1)
    blocks = v.reshape(v.shape[:-1] + (-1, 32))
    amax = np.abs(blocks).max(-1, keepdims=True)
    byte = np.maximum(np.where(amax > 0, np.frexp(amax)[1] - 1 + 127, 0) - down, 1)
    scale = np.exp2(byte - 127.0)
    codes = (blocks / scale).astype(np.float32).astype(dtype).astype(np.float64)
    return np.moveaxis((codes * scale).reshape(v.shape), -1, axis)


WIDE = False


def mx_kscale(k):
    if not WIDE:
        return np.ones(k)
    levels = np.array([10, -10, 5, -5, 0])
    a = np.random.permutation(np.resize(levels, k // 512 * 4)).reshape(k // 512, 4)
    idx = np.arange(k)
    return np.exp2(a[idx // 512, idx % 128 // 32])


BF16 = ml_dtypes.bfloat16


def bf(x):
    return np.asarray(x, np.float32).astype(BF16)


def f64(x):
    return np.asarray(x).astype(np.float64)


B, IN_F, FEAT, NCLASS = 256, 1024, 128, 256
D = 4 * FEAT
GAMMA = 0.1


def setup_inputs():
    s = mx_kscale(IN_F)
    ws = 0.5 / np.sqrt(IN_F)
    return {
        "x": bf(np.random.standard_normal((B, IN_F)) * s),
        "x_90": bf(np.random.standard_normal((B, IN_F)) * s),
        "x_180": bf(np.random.standard_normal((B, IN_F)) * s),
        "x_270": bf(np.random.standard_normal((B, IN_F)) * s),
        "W_f": bf(np.random.standard_normal((FEAT, IN_F)) * ws / s),
        "b_f": bf(np.random.standard_normal(FEAT) * 0.25),
        "W_r": bf(np.random.standard_normal((FEAT, IN_F)) * ws / s),
        "b_r": bf(np.random.standard_normal(FEAT) * 0.25),
        "centers": bf(0.2 + 0.3 * np.random.standard_normal((NCLASS, D))),
    }


def reference(x, x_90, x_180, x_270, W_f, b_f, W_r, b_r, centers):
    wf = mxq(f64(W_f), 1, "e4m3")
    wr = mxq(f64(W_r), 1, "e4m3")
    f = np.maximum((mxq(f64(x), 1, "e4m3") @ wf.T) + f64(b_f), 0.0)
    f90 = np.maximum((mxq(f64(x_90), 1, "e4m3") @ wr.T) + f64(b_r), 0.0)
    f180 = np.maximum((mxq(f64(x_180), 1, "e4m3") @ wr.T) + f64(b_r), 0.0)
    f270 = np.maximum((mxq(f64(x_270), 1, "e4m3") @ wr.T) + f64(b_r), 0.0)
    feat = np.concatenate((f, f90, f180, f270), axis=1)
    c = f64(centers)
    f2 = np.sum(feat * feat, axis=1, keepdims=True)
    c2 = np.sum(c * c, axis=1)
    d2 = f2 + c2[None, :] - 2.0 * (mxq(feat, 1, "e4m3") @ mxq(c, 1, "e4m3").T)
    return np.sqrt(np.maximum(d2, 0.0)) * (-GAMMA)

@@ -1,0 +1,192 @@
+from contextlib import ExitStack
+
+import concourse.mybir as mybir
+from concourse.masks import make_identity
+
+F32 = mybir.dt.float32
+BF16 = mybir.dt.bfloat16
+U32 = mybir.dt.uint32
+U8 = mybir.dt.uint8
+FP8X4 = mybir.dt.float8_e4m3fn_x4
+ALU = mybir.AluOpType
+ACT = mybir.ActivationFunctionType
+
+P = 128
+PACK = 4
+HALVES = 2
+K_PASS = P * PACK
+
+BATCH, IN_F, FEAT, NCLASS = 256, 1024, 128, 256
+VIEWS = 4
+JOINED = VIEWS * FEAT
+PASSES = IN_F // K_PASS
+ROW_BLOCKS = BATCH // P
+CLASS_BLOCKS = NCLASS // P
+GAMMA = 0.1
+
+FLOPS = 2 * BATCH * IN_F * FEAT * VIEWS + 2 * BATCH * JOINED * NCLASS
+
+
+def quantise_rows(nc, copy_out, flip_pool, stage_pool, rows_sb, ident_f32, codes, scales):
+    pairs = rows_sb[:].bitcast(F32)
+    flipped = flip_pool.tile([P, PASSES, HALVES, P], F32, tag="flipped")
+    for g in range(PASSES):
+        for u in range(HALVES):
+            first = (g * HALVES + u) * P
+            nc.tensor.transpose(flipped[:, g, u, :], pairs[:, first : first + P], ident_f32[:])
+    grouped = stage_pool.tile([P, PASSES * P * PACK], BF16, align_bytes=64, tag="grouped")
+    copy_out(
+        out=grouped[:].bitcast(F32).rearrange("p (g r u) -> p g r u", g=PASSES, u=HALVES),
+        in_=flipped[:].rearrange("p g u r -> p g r u"),
+    )
+    nc.vector.quantize_mx(out=codes.bitcast(FP8X4), scales=scales, in_=grouped[:])
+
+
+def tile_qccpn_pa_s_kernel(tc, x, x_90, x_180, x_270, W_f, b_f, W_r, b_r, centers, out):
+    nc = tc.nc
+    views = [x, x_90, x_180, x_270]
+    weight_of_view = [0, 1, 1, 1]
+
+    with ExitStack() as stack:
+        const = stack.enter_context(tc.tile_pool(name="const", bufs=1))
+        rows_pool = stack.enter_context(tc.tile_pool(name="rows", bufs=VIEWS * ROW_BLOCKS))
+        stage = stack.enter_context(tc.tile_pool(name="stage", bufs=3))
+        flip_pool = stack.enter_context(tc.psum_pool(name="flip", bufs=3))
+        feat_t_pool = stack.enter_context(tc.psum_pool(name="feat_t", bufs=2))
+        feat_n_pool = stack.enter_context(tc.psum_pool(name="feat_n", bufs=1))
+        dot_pool = stack.enter_context(tc.psum_pool(name="dot", bufs=2))
+
+        bias_bf = [const.tile([FEAT, 1], BF16, name="bias_bf%d" % w) for w in range(2)]
+        with nc.allow_non_contiguous_dma(reason="a bias of 128 values, one to a partition"):
+            for w, b_dram in enumerate([b_f, b_r]):
+                nc.scalar.dma_start(out=bias_bf[w][:], in_=b_dram.rearrange("(f o) -> f o", o=1))
+
+        w_rows = [const.tile([FEAT, IN_F], BF16, name="w_rows%d" % w) for w in range(2)]
+        x_rows = {}
+        for b in range(ROW_BLOCKS):
+            for v in range(VIEWS):
+                x_rows[(b, v)] = rows_pool.tile([P, IN_F], BF16, name="x_rows", tag="x_rows")
+        cen_rows = const.tile([P, CLASS_BLOCKS, JOINED], BF16)
+
+        def load_x(b, v):
+            nc.sync.dma_start(out=x_rows[(b, v)][:], in_=views[v][b * P : (b + 1) * P, :])
+
+        nc.sync.dma_start(out=w_rows[0][:], in_=W_f)
+        load_x(0, 0)
+        nc.sync.dma_start(out=w_rows[1][:], in_=W_r)
+        for v in range(1, VIEWS):
+            load_x(0, v)
+        nc.sync.dma_start(out=cen_rows[:], in_=centers.rearrange("(cb c) j -> c cb j", c=P))
+        for v in range(VIEWS):
+            load_x(1, v)
+
+        ident_f32 = const.tile([P, P], F32)
+        make_identity(nc, ident_f32[:])
+        ident_bf = const.tile([P, P], BF16)
+        nc.vector.tensor_copy(out=ident_bf[:], in_=ident_f32[:])
+        one = const.tile([P, 1], F32)
+        nc.vector.memset(one[:], 1.0)
+        one_root = const.tile([P, 1], F32)
+        nc.scalar.activation(out=one_root[:], in_=one[:], func=ACT.Sqrt)
+        bias = [const.tile([FEAT, 1], F32, name="bias%d" % w) for w in range(2)]
+        for w in range(2):
+            nc.vector.tensor_copy(out=bias[w][:], in_=bias_bf[w][:])
+
+        w_codes = [const.tile([P, PASSES * FEAT], U32, align_bytes=64, name="w_codes%d" % w) for w in range(2)]
+        w_scales = [const.tile([P, PASSES * FEAT], U8, align_bytes=64, name="w_scales%d" % w) for w in range(2)]
+        for w in range(2):
+            quantise_rows(nc, nc.vector.tensor_copy, flip_pool, stage, w_rows[w], ident_f32, w_codes[w][:], w_scales[w][:])
+
+        cen_flipped = dot_pool.tile([P, CLASS_BLOCKS, VIEWS, P], BF16, tag="dot")
+        for cb in range(CLASS_BLOCKS):
+            for v in range(VIEWS):
+                nc.tensor.transpose(cen_flipped[:, cb, v, :], cen_rows[:, cb, v * P : (v + 1) * P], ident_bf[:])
+        cen_grouped = const.tile([P, NCLASS * PACK], BF16, align_bytes=64)
+        nc.vector.tensor_copy(
+            out=cen_grouped[:].rearrange("p (cb c v) -> p cb c v", cb=CLASS_BLOCKS, v=VIEWS),
+            in_=cen_flipped[:].rearrange("p cb v c -> p cb c v"),
+        )
+        cen_codes = const.tile([P, NCLASS], U32, align_bytes=64)
+        cen_scales = const.tile([P, NCLASS], U8, align_bytes=64)
+        nc.vector.quantize_mx(out=cen_codes[:].bitcast(FP8X4), scales=cen_scales[:], in_=cen_grouped[:])
+
+        c2_col = const.tile([P, CLASS_BLOCKS], F32)
+        cen_squares = const.tile([P, CLASS_BLOCKS, JOINED], F32)
+        c2_spread = dot_pool.tile([P, NCLASS], F32, tag="dot")
+        for cb in range(CLASS_BLOCKS):
+            nc.scalar.activation(
+                out=cen_squares[:, cb, :], in_=cen_rows[:, cb, :], func=ACT.Square, accum_out=c2_col[:, cb : cb + 1]
+            )
+            nc.tensor.matmul(
+                out=c2_spread[:, cb * P : (cb + 1) * P],
+                lhsT=c2_col[:, cb : cb + 1].to_broadcast([P, P]),
+                rhs=ident_f32[:],
+                start=True,
+                stop=True,
+            )
+        c2_all = const.tile([P, NCLASS], F32)
+        nc.vector.tensor_copy(out=c2_all[:], in_=c2_spread[:])
+
+        for b in range(ROW_BLOCKS):
+            feat_grouped = stage.tile([P, P, VIEWS], BF16, align_bytes=64)
+            feat_rows = feat_n_pool.tile([P, VIEWS, FEAT], F32)
+            for v in range(VIEWS):
+                w = weight_of_view[v]
+                x_codes = stage.tile([P, PASSES * P], U32, align_bytes=64)
+                x_scales = stage.tile([P, PASSES * P], U8, align_bytes=64)
+                quantise_rows(nc, nc.scalar.copy, flip_pool, stage, x_rows[(b, v)], ident_f32, x_codes[:], x_scales[:])
+
+                feat_t = feat_t_pool.tile([FEAT, P], F32)
+                for g in range(PASSES):
+                    cols = slice(g * P, (g + 1) * P)
+                    nc.tensor.matmul_mx(
+                        out=feat_t[:],
+                        lhsT=w_codes[w][:, cols].bitcast(FP8X4),
+                        lhsT_scale=w_scales[w][:, cols],
+                        rhs=x_codes[:, cols].bitcast(FP8X4),
+                        rhs_scale=x_scales[:, cols],
+                        start=(g == 0),
+                        stop=(g == PASSES - 1),
+                    )
+                feat = stage.tile([FEAT, P], F32)
+                nc.vector.tensor_scalar(
+                    out=feat[:], in0=feat_t[:], scalar1=bias[w][:, 0:1], scalar2=0.0, op0=ALU.add, op1=ALU.max
+                )
+                nc.vector.tensor_copy(out=feat_grouped[:, :, v], in_=feat[:])
+                nc.tensor.transpose(feat_rows[:, v, :], feat[:], ident_f32[:])
+
+            f2 = stage.tile([P, 1], F32)
+            feat_squares = stage.tile([P, JOINED], F32)
+            nc.scalar.activation(
+                out=feat_squares[:], in_=feat_rows[:].rearrange("i v f -> i (v f)"), func=ACT.Square, accum_out=f2[:]
+            )
+
+            feat_codes = stage.tile([P, P], U32, align_bytes=64)
+            feat_scales = stage.tile([P, P], U8, align_bytes=64)
+            nc.vector.quantize_mx(
+                out=feat_codes[:].bitcast(FP8X4), scales=feat_scales[:], in_=feat_grouped[:].rearrange("p i v -> p (i v)")
+            )
+            dot = dot_pool.tile([P, NCLASS], F32, tag="dot")
+            nc.tensor.matmul_mx(
+                out=dot[:],
+                lhsT=feat_codes[:].bitcast(FP8X4),
+                lhsT_scale=feat_scales[:],
+                rhs=cen_codes[:].bitcast(FP8X4),
+                rhs_scale=cen_scales[:],
+                start=True,
+                stop=True,
+            )
+
+            partial = stage.tile([P, NCLASS], F32)
+            nc.vector.scalar_tensor_tensor(
+                out=partial[:], in0=dot[:], scalar=-2.0, in1=c2_all[:], op0=ALU.mult, op1=ALU.add
+            )
+            d2 = stage.tile([P, NCLASS], F32)
+            nc.vector.tensor_scalar(
+                out=d2[:], in0=partial[:], scalar1=f2[:, 0:1], scalar2=0.0, op0=ALU.add, op1=ALU.max
+            )
+            root = stage.tile([P, NCLASS], F32)
+            nc.scalar.activation(out=root[:], in_=d2[:], func=ACT.Sqrt)
+            score = stage.tile([P, NCLASS], F32)
+            nc.vector.tensor_scalar_mul(out=score[:], in0=root[:], scalar1=-GAMMA)
+            nc.sync.dma_start(out=out[b * P : (b + 1) * P, :], in_=score[:])

@@ -48,13 +48,16 @@ def tile_qccpn_pa_s_kernel(tc, x, x_90, x_180, x_270, W_f, b_f, W_r, b_r, center
     weight_of_view = [0, 1, 1, 1]
 
     with ExitStack() as stack:
+        stack.enter_context(tc.manual_schedule())
         const = stack.enter_context(tc.tile_pool(name="const", bufs=1))
         rows_pool = stack.enter_context(tc.tile_pool(name="rows", bufs=VIEWS * ROW_BLOCKS))
         stage = stack.enter_context(tc.tile_pool(name="stage", bufs=3))
+        per_view = stack.enter_context(tc.tile_pool(name="per_view", bufs=VIEWS))
+        per_block = stack.enter_context(tc.tile_pool(name="per_block", bufs=ROW_BLOCKS))
         flip_pool = stack.enter_context(tc.psum_pool(name="flip", bufs=3))
         feat_t_pool = stack.enter_context(tc.psum_pool(name="feat_t", bufs=2))
         feat_n_pool = stack.enter_context(tc.psum_pool(name="feat_n", bufs=1))
-        dot_pool = stack.enter_context(tc.psum_pool(name="dot", bufs=2))
+        dot_pool = stack.enter_context(tc.psum_pool(name="dot", bufs=ROW_BLOCKS))
 
         bias_bf = [const.tile([FEAT, 1], BF16, name="bias_bf%d" % w) for w in range(2)]
         with nc.allow_non_contiguous_dma(reason="a bias of 128 values, one to a partition"):
@@ -80,24 +83,85 @@ def tile_qccpn_pa_s_kernel(tc, x, x_90, x_180, x_270, W_f, b_f, W_r, b_r, center
         for v in range(VIEWS):
             load_x(1, v)
 
-        ident_f32 = const.tile([P, P], F32)
-        make_identity(nc, ident_f32[:])
-        ident_bf = const.tile([P, P], BF16)
-        nc.vector.tensor_copy(out=ident_bf[:], in_=ident_f32[:])
         one = const.tile([P, 1], F32)
         nc.vector.memset(one[:], 1.0)
         one_root = const.tile([P, 1], F32)
         nc.scalar.activation(out=one_root[:], in_=one[:], func=ACT.Sqrt)
-        bias = [const.tile([FEAT, 1], F32, name="bias%d" % w) for w in range(2)]
-        for w in range(2):
-            nc.vector.tensor_copy(out=bias[w][:], in_=bias_bf[w][:])
+        ident_f32 = const.tile([P, P], F32)
+        make_identity(nc, ident_f32[:])
+        ident_bf = const.tile([P, P], BF16)
+        nc.vector.tensor_copy(out=ident_bf[:], in_=ident_f32[:])
 
         w_codes = [const.tile([P, PASSES * FEAT], U32, align_bytes=64, name="w_codes%d" % w) for w in range(2)]
         w_scales = [const.tile([P, PASSES * FEAT], U8, align_bytes=64, name="w_scales%d" % w) for w in range(2)]
-        for w in range(2):
+        x_codes, x_scales, feat, feat_grouped, f2, feat_codes, feat_scales, dot, root = {}, {}, {}, {}, {}, {}, {}, {}, {}
+
+        def quantise_weight(w):
             quantise_rows(nc, nc.vector.tensor_copy, flip_pool, stage, w_rows[w], ident_f32, w_codes[w][:], w_scales[w][:])
 
-        cen_flipped = dot_pool.tile([P, CLASS_BLOCKS, VIEWS, P], BF16, tag="dot")
+        def quantise_view(b, v):
+            x_codes[v] = per_view.tile([P, PASSES * P], U32, align_bytes=64, name="x_codes")
+            x_scales[v] = per_view.tile([P, PASSES * P], U8, align_bytes=64, name="x_scales")
+            quantise_rows(nc, nc.scalar.copy, flip_pool, stage, x_rows[(b, v)], ident_f32, x_codes[v][:], x_scales[v][:])
+
+        def project(b, v):
+            w = weight_of_view[v]
+            feat_t = feat_t_pool.tile([FEAT, P], F32)
+            for g in range(PASSES):
+                cols = slice(g * P, (g + 1) * P)
+                nc.tensor.matmul_mx(
+                    out=feat_t[:],
+                    lhsT=w_codes[w][:, cols].bitcast(FP8X4),
+                    lhsT_scale=w_scales[w][:, cols],
+                    rhs=x_codes[v][:, cols].bitcast(FP8X4),
+                    rhs_scale=x_scales[v][:, cols],
+                    start=(g == 0),
+                    stop=(g == PASSES - 1),
+                )
+            feat[v] = per_view.tile([FEAT, P], F32, name="feat")
+            nc.scalar.activation(out=feat[v][:], in_=feat_t[:], func=ACT.Relu, bias=bias[w][:, 0:1])
+            nc.vector.tensor_copy(out=feat_grouped[b][:, :, v], in_=feat[v][:])
+
+        def quantise_features(b):
+            feat_codes[b] = per_block.tile([P, P], U32, align_bytes=64, name="feat_codes")
+            feat_scales[b] = per_block.tile([P, P], U8, align_bytes=64, name="feat_scales")
+            nc.vector.quantize_mx(
+                out=feat_codes[b][:].bitcast(FP8X4),
+                scales=feat_scales[b][:],
+                in_=feat_grouped[b][:].rearrange("p i v -> p (i v)"),
+            )
+
+        def sum_squared_features(b):
+            feat_rows = feat_n_pool.tile([P, VIEWS, FEAT], F32)
+            for v in range(VIEWS):
+                nc.tensor.transpose(feat_rows[:, v, :], feat[v][:], ident_f32[:])
+            f2[b] = per_block.tile([P, 1], F32, name="f2")
+            feat_squares = stage.tile([P, JOINED], F32)
+            nc.scalar.activation(
+                out=feat_squares[:], in_=feat_rows[:].rearrange("i v f -> i (v f)"), func=ACT.Square, accum_out=f2[b][:]
+            )
+
+        def multiply_by_centers(b):
+            dot[b] = dot_pool.tile([P, NCLASS], F32, name="dot")
+            nc.tensor.matmul_mx(
+                out=dot[b][:],
+                lhsT=feat_codes[b][:].bitcast(FP8X4),
+                lhsT_scale=feat_scales[b][:],
+                rhs=cen_codes[:].bitcast(FP8X4),
+                rhs_scale=cen_scales[:],
+                start=True,
+                stop=True,
+            )
+
+        for b in range(ROW_BLOCKS):
+            feat_grouped[b] = per_block.tile([P, P, VIEWS], BF16, align_bytes=64, name="feat_grouped")
+        quantise_weight(0)
+        quantise_view(0, 0)
+        quantise_weight(1)
+        for v in range(1, VIEWS):
+            quantise_view(0, v)
+
+        cen_flipped = flip_pool.tile([P, CLASS_BLOCKS, VIEWS, P], BF16, tag="flipped")
         for cb in range(CLASS_BLOCKS):
             for v in range(VIEWS):
                 nc.tensor.transpose(cen_flipped[:, cb, v, :], cen_rows[:, cb, v * P : (v + 1) * P], ident_bf[:])
@@ -110,83 +174,53 @@ def tile_qccpn_pa_s_kernel(tc, x, x_90, x_180, x_270, W_f, b_f, W_r, b_r, center
         cen_scales = const.tile([P, NCLASS], U8, align_bytes=64)
         nc.vector.quantize_mx(out=cen_codes[:].bitcast(FP8X4), scales=cen_scales[:], in_=cen_grouped[:])
 
+        bias = [const.tile([FEAT, 1], F32, name="bias%d" % w) for w in range(2)]
+        for w in range(2):
+            nc.vector.tensor_copy(out=bias[w][:], in_=bias_bf[w][:])
+
         c2_col = const.tile([P, CLASS_BLOCKS], F32)
         cen_squares = const.tile([P, CLASS_BLOCKS, JOINED], F32)
-        c2_spread = dot_pool.tile([P, NCLASS], F32, tag="dot")
         for cb in range(CLASS_BLOCKS):
             nc.scalar.activation(
                 out=cen_squares[:, cb, :], in_=cen_rows[:, cb, :], func=ACT.Square, accum_out=c2_col[:, cb : cb + 1]
             )
-            nc.tensor.matmul(
-                out=c2_spread[:, cb * P : (cb + 1) * P],
-                lhsT=c2_col[:, cb : cb + 1].to_broadcast([P, P]),
-                rhs=ident_f32[:],
-                start=True,
-                stop=True,
-            )
+        c2_repeated = const.tile([P, CLASS_BLOCKS, P], F32)
+        nc.vector.tensor_copy(out=c2_repeated[:], in_=c2_col[:].unsqueeze(2).to_broadcast([P, CLASS_BLOCKS, P]))
+
+        for v in range(VIEWS):
+            project(0, v)
+        quantise_features(0)
+
+        for v in range(VIEWS):
+            quantise_view(1, v)
+        sum_squared_features(0)
+        c2_spread = flip_pool.tile([P, NCLASS], F32, tag="flipped")
+        for cb in range(CLASS_BLOCKS):
+            nc.tensor.transpose(c2_spread[:, cb * P : (cb + 1) * P], c2_repeated[:, cb, :], ident_f32[:])
         c2_all = const.tile([P, NCLASS], F32)
         nc.vector.tensor_copy(out=c2_all[:], in_=c2_spread[:])
 
+        for v in range(VIEWS):
+            project(1, v)
+        multiply_by_centers(0)
+
+        sum_squared_features(1)
+        quantise_features(1)
+
+        multiply_by_centers(1)
+
         for b in range(ROW_BLOCKS):
-            feat_grouped = stage.tile([P, P, VIEWS], BF16, align_bytes=64)
-            feat_rows = feat_n_pool.tile([P, VIEWS, FEAT], F32)
-            for v in range(VIEWS):
-                w = weight_of_view[v]
-                x_codes = stage.tile([P, PASSES * P], U32, align_bytes=64)
-                x_scales = stage.tile([P, PASSES * P], U8, align_bytes=64)
-                quantise_rows(nc, nc.scalar.copy, flip_pool, stage, x_rows[(b, v)], ident_f32, x_codes[:], x_scales[:])
-
-                feat_t = feat_t_pool.tile([FEAT, P], F32)
-                for g in range(PASSES):
-                    cols = slice(g * P, (g + 1) * P)
-                    nc.tensor.matmul_mx(
-                        out=feat_t[:],
-                        lhsT=w_codes[w][:, cols].bitcast(FP8X4),
-                        lhsT_scale=w_scales[w][:, cols],
-                        rhs=x_codes[:, cols].bitcast(FP8X4),
-                        rhs_scale=x_scales[:, cols],
-                        start=(g == 0),
-                        stop=(g == PASSES - 1),
-                    )
-                feat = stage.tile([FEAT, P], F32)
-                nc.vector.tensor_scalar(
-                    out=feat[:], in0=feat_t[:], scalar1=bias[w][:, 0:1], scalar2=0.0, op0=ALU.add, op1=ALU.max
-                )
-                nc.vector.tensor_copy(out=feat_grouped[:, :, v], in_=feat[:])
-                nc.tensor.transpose(feat_rows[:, v, :], feat[:], ident_f32[:])
-
-            f2 = stage.tile([P, 1], F32)
-            feat_squares = stage.tile([P, JOINED], F32)
-            nc.scalar.activation(
-                out=feat_squares[:], in_=feat_rows[:].rearrange("i v f -> i (v f)"), func=ACT.Square, accum_out=f2[:]
-            )
-
-            feat_codes = stage.tile([P, P], U32, align_bytes=64)
-            feat_scales = stage.tile([P, P], U8, align_bytes=64)
-            nc.vector.quantize_mx(
-                out=feat_codes[:].bitcast(FP8X4), scales=feat_scales[:], in_=feat_grouped[:].rearrange("p i v -> p (i v)")
-            )
-            dot = dot_pool.tile([P, NCLASS], F32, tag="dot")
-            nc.tensor.matmul_mx(
-                out=dot[:],
-                lhsT=feat_codes[:].bitcast(FP8X4),
-                lhsT_scale=feat_scales[:],
-                rhs=cen_codes[:].bitcast(FP8X4),
-                rhs_scale=cen_scales[:],
-                start=True,
-                stop=True,
-            )
-
             partial = stage.tile([P, NCLASS], F32)
             nc.vector.scalar_tensor_tensor(
-                out=partial[:], in0=dot[:], scalar=-2.0, in1=c2_all[:], op0=ALU.mult, op1=ALU.add
+                out=partial[:], in0=dot[b][:], scalar=-2.0, in1=c2_all[:], op0=ALU.mult, op1=ALU.add
             )
             d2 = stage.tile([P, NCLASS], F32)
             nc.vector.tensor_scalar(
-                out=d2[:], in0=partial[:], scalar1=f2[:, 0:1], scalar2=0.0, op0=ALU.add, op1=ALU.max
+                out=d2[:], in0=partial[:], scalar1=f2[b][:, 0:1], scalar2=0.0, op0=ALU.add, op1=ALU.max
             )
-            root = stage.tile([P, NCLASS], F32)
-            nc.scalar.activation(out=root[:], in_=d2[:], func=ACT.Sqrt)
+            root[b] = per_block.tile([P, NCLASS], F32, name="root")
+            nc.scalar.activation(out=root[b][:], in_=d2[:], func=ACT.Sqrt)
+        for b in range(ROW_BLOCKS):
             score = stage.tile([P, NCLASS], F32)
-            nc.vector.tensor_scalar_mul(out=score[:], in0=root[:], scalar1=-GAMMA)
+            nc.vector.tensor_scalar_mul(out=score[:], in0=root[b][:], scalar1=-GAMMA)
             nc.sync.dma_start(out=out[b * P : (b + 1) * P, :], in_=score[:])

@@ -23,13 +23,14 @@ PASSES = IN_F // K_PASS
 ROW_BLOCKS = BATCH // P
 CLASS_BLOCKS = NCLASS // P
 GAMMA = 0.1
+PSUM_BANKS = 8
 
 FLOPS = 2 * BATCH * IN_F * FEAT * VIEWS + 2 * BATCH * JOINED * NCLASS
 
 
-def quantise_rows(nc, copy_out, flip_pool, stage_pool, rows_sb, ident_f32, codes, scales):
+def quantise_rows(nc, copy_out, psum, stage_pool, rows_sb, ident_f32, codes, scales):
     pairs = rows_sb[:].bitcast(F32)
-    flipped = flip_pool.tile([P, PASSES, HALVES, P], F32, tag="flipped")
+    flipped = psum.tile([P, PASSES, HALVES, P], F32, tag="bank")
     for g in range(PASSES):
         for u in range(HALVES):
             first = (g * HALVES + u) * P
@@ -52,12 +53,9 @@ def tile_qccpn_pa_s_kernel(tc, x, x_90, x_180, x_270, W_f, b_f, W_r, b_r, center
         const = stack.enter_context(tc.tile_pool(name="const", bufs=1))
         rows_pool = stack.enter_context(tc.tile_pool(name="rows", bufs=VIEWS * ROW_BLOCKS))
         stage = stack.enter_context(tc.tile_pool(name="stage", bufs=3))
-        per_view = stack.enter_context(tc.tile_pool(name="per_view", bufs=VIEWS))
+        per_view = stack.enter_context(tc.tile_pool(name="per_view", bufs=VIEWS * ROW_BLOCKS))
         per_block = stack.enter_context(tc.tile_pool(name="per_block", bufs=ROW_BLOCKS))
-        flip_pool = stack.enter_context(tc.psum_pool(name="flip", bufs=3))
-        feat_t_pool = stack.enter_context(tc.psum_pool(name="feat_t", bufs=2))
-        feat_n_pool = stack.enter_context(tc.psum_pool(name="feat_n", bufs=1))
-        dot_pool = stack.enter_context(tc.psum_pool(name="dot", bufs=ROW_BLOCKS))
+        psum = stack.enter_context(tc.psum_pool(name="psum", bufs=PSUM_BANKS))
 
         bias_bf = [const.tile([FEAT, 1], BF16, name="bias_bf%d" % w) for w in range(2)]
         with nc.allow_non_contiguous_dma(reason="a bias of 128 values, one to a partition"):
@@ -74,12 +72,13 @@ def tile_qccpn_pa_s_kernel(tc, x, x_90, x_180, x_270, W_f, b_f, W_r, b_r, center
         def load_x(b, v):
             nc.sync.dma_start(out=x_rows[(b, v)][:], in_=views[v][b * P : (b + 1) * P, :])
 
+        for cb in range(CLASS_BLOCKS):
+            nc.sync.dma_start(out=cen_rows[:, cb, :], in_=centers[cb * P : (cb + 1) * P, :])
         nc.sync.dma_start(out=w_rows[0][:], in_=W_f)
         load_x(0, 0)
         nc.sync.dma_start(out=w_rows[1][:], in_=W_r)
         for v in range(1, VIEWS):
             load_x(0, v)
-        nc.sync.dma_start(out=cen_rows[:], in_=centers.rearrange("(cb c) j -> c cb j", c=P))
         for v in range(VIEWS):
             load_x(1, v)
 
@@ -96,31 +95,42 @@ def tile_qccpn_pa_s_kernel(tc, x, x_90, x_180, x_270, W_f, b_f, W_r, b_r, center
         w_scales = [const.tile([P, PASSES * FEAT], U8, align_bytes=64, name="w_scales%d" % w) for w in range(2)]
         x_codes, x_scales, feat, feat_grouped, f2, feat_codes, feat_scales, dot, root = {}, {}, {}, {}, {}, {}, {}, {}, {}
 
+        banks_emptied = []
+
+        def copy_out(out, in_):
+            if len(banks_emptied) % 3 == 0:
+                nc.vector.tensor_copy(out=out, in_=in_)
+            else:
+                nc.scalar.copy(out=out, in_=in_)
+            banks_emptied.append(1)
+
         def quantise_weight(w):
-            quantise_rows(nc, nc.vector.tensor_copy, flip_pool, stage, w_rows[w], ident_f32, w_codes[w][:], w_scales[w][:])
+            quantise_rows(nc, copy_out, psum, stage, w_rows[w], ident_f32, w_codes[w][:], w_scales[w][:])
 
         def quantise_view(b, v):
-            x_codes[v] = per_view.tile([P, PASSES * P], U32, align_bytes=64, name="x_codes")
-            x_scales[v] = per_view.tile([P, PASSES * P], U8, align_bytes=64, name="x_scales")
-            quantise_rows(nc, nc.scalar.copy, flip_pool, stage, x_rows[(b, v)], ident_f32, x_codes[v][:], x_scales[v][:])
+            x_codes[(b, v)] = per_view.tile([P, PASSES * P], U32, align_bytes=64, name="x_codes")
+            x_scales[(b, v)] = per_view.tile([P, PASSES * P], U8, align_bytes=64, name="x_scales")
+            quantise_rows(
+                nc, copy_out, psum, stage, x_rows[(b, v)], ident_f32, x_codes[(b, v)][:], x_scales[(b, v)][:]
+            )
 
         def project(b, v):
             w = weight_of_view[v]
-            feat_t = feat_t_pool.tile([FEAT, P], F32)
+            feat_t = psum.tile([FEAT, P], F32, tag="bank")
             for g in range(PASSES):
                 cols = slice(g * P, (g + 1) * P)
                 nc.tensor.matmul_mx(
                     out=feat_t[:],
                     lhsT=w_codes[w][:, cols].bitcast(FP8X4),
                     lhsT_scale=w_scales[w][:, cols],
-                    rhs=x_codes[v][:, cols].bitcast(FP8X4),
-                    rhs_scale=x_scales[v][:, cols],
+                    rhs=x_codes[(b, v)][:, cols].bitcast(FP8X4),
+                    rhs_scale=x_scales[(b, v)][:, cols],
                     start=(g == 0),
                     stop=(g == PASSES - 1),
                 )
-            feat[v] = per_view.tile([FEAT, P], F32, name="feat")
-            nc.scalar.activation(out=feat[v][:], in_=feat_t[:], func=ACT.Relu, bias=bias[w][:, 0:1])
-            nc.vector.tensor_copy(out=feat_grouped[b][:, :, v], in_=feat[v][:])
+            feat[(b, v)] = per_view.tile([FEAT, P], F32, name="feat")
+            nc.scalar.activation(out=feat[(b, v)][:], in_=feat_t[:], func=ACT.Relu, bias=bias[w][:, 0:1])
+            nc.vector.tensor_copy(out=feat_grouped[b][:, :, v], in_=feat[(b, v)][:])
 
         def quantise_features(b):
             feat_codes[b] = per_block.tile([P, P], U32, align_bytes=64, name="feat_codes")
@@ -132,9 +142,9 @@ def tile_qccpn_pa_s_kernel(tc, x, x_90, x_180, x_270, W_f, b_f, W_r, b_r, center
             )
 
         def sum_squared_features(b):
-            feat_rows = feat_n_pool.tile([P, VIEWS, FEAT], F32)
+            feat_rows = psum.tile([P, VIEWS, FEAT], F32, tag="bank")
             for v in range(VIEWS):
-                nc.tensor.transpose(feat_rows[:, v, :], feat[v][:], ident_f32[:])
+                nc.tensor.transpose(feat_rows[:, v, :], feat[(b, v)][:], ident_f32[:])
             f2[b] = per_block.tile([P, 1], F32, name="f2")
             feat_squares = stage.tile([P, JOINED], F32)
             nc.scalar.activation(
@@ -142,7 +152,7 @@ def tile_qccpn_pa_s_kernel(tc, x, x_90, x_180, x_270, W_f, b_f, W_r, b_r, center
             )
 
         def multiply_by_centers(b):
-            dot[b] = dot_pool.tile([P, NCLASS], F32, name="dot")
+            dot[b] = psum.tile([P, NCLASS], F32, name="dot", tag="bank")
             nc.tensor.matmul_mx(
                 out=dot[b][:],
                 lhsT=feat_codes[b][:].bitcast(FP8X4),
@@ -155,28 +165,18 @@ def tile_qccpn_pa_s_kernel(tc, x, x_90, x_180, x_270, W_f, b_f, W_r, b_r, center
 
         for b in range(ROW_BLOCKS):
             feat_grouped[b] = per_block.tile([P, P, VIEWS], BF16, align_bytes=64, name="feat_grouped")
-        quantise_weight(0)
-        quantise_view(0, 0)
-        quantise_weight(1)
-        for v in range(1, VIEWS):
-            quantise_view(0, v)
-
-        cen_flipped = flip_pool.tile([P, CLASS_BLOCKS, VIEWS, P], BF16, tag="flipped")
+        cen_flipped = psum.tile([P, CLASS_BLOCKS, VIEWS, P], BF16, tag="bank")
         for cb in range(CLASS_BLOCKS):
             for v in range(VIEWS):
                 nc.tensor.transpose(cen_flipped[:, cb, v, :], cen_rows[:, cb, v * P : (v + 1) * P], ident_bf[:])
         cen_grouped = const.tile([P, NCLASS * PACK], BF16, align_bytes=64)
-        nc.vector.tensor_copy(
+        copy_out(
             out=cen_grouped[:].rearrange("p (cb c v) -> p cb c v", cb=CLASS_BLOCKS, v=VIEWS),
             in_=cen_flipped[:].rearrange("p cb v c -> p cb c v"),
         )
         cen_codes = const.tile([P, NCLASS], U32, align_bytes=64)
         cen_scales = const.tile([P, NCLASS], U8, align_bytes=64)
         nc.vector.quantize_mx(out=cen_codes[:].bitcast(FP8X4), scales=cen_scales[:], in_=cen_grouped[:])
-
-        bias = [const.tile([FEAT, 1], F32, name="bias%d" % w) for w in range(2)]
-        for w in range(2):
-            nc.vector.tensor_copy(out=bias[w][:], in_=bias_bf[w][:])
 
         c2_col = const.tile([P, CLASS_BLOCKS], F32)
         cen_squares = const.tile([P, CLASS_BLOCKS, JOINED], F32)
@@ -187,27 +187,33 @@ def tile_qccpn_pa_s_kernel(tc, x, x_90, x_180, x_270, W_f, b_f, W_r, b_r, center
         c2_repeated = const.tile([P, CLASS_BLOCKS, P], F32)
         nc.vector.tensor_copy(out=c2_repeated[:], in_=c2_col[:].unsqueeze(2).to_broadcast([P, CLASS_BLOCKS, P]))
 
-        for v in range(VIEWS):
-            project(0, v)
-        quantise_features(0)
-
+        quantise_weight(0)
+        quantise_view(0, 0)
+        quantise_weight(1)
+        for v in range(1, VIEWS):
+            quantise_view(0, v)
         for v in range(VIEWS):
             quantise_view(1, v)
-        sum_squared_features(0)
-        c2_spread = flip_pool.tile([P, NCLASS], F32, tag="flipped")
+
+        bias = [const.tile([FEAT, 1], F32, name="bias%d" % w) for w in range(2)]
+        for w in range(2):
+            nc.vector.tensor_copy(out=bias[w][:], in_=bias_bf[w][:])
+
+        for b in range(ROW_BLOCKS):
+            for v in range(VIEWS):
+                project(b, v)
+            quantise_features(b)
+
+        c2_spread = psum.tile([P, NCLASS], F32, tag="bank")
         for cb in range(CLASS_BLOCKS):
             nc.tensor.transpose(c2_spread[:, cb * P : (cb + 1) * P], c2_repeated[:, cb, :], ident_f32[:])
         c2_all = const.tile([P, NCLASS], F32)
         nc.vector.tensor_copy(out=c2_all[:], in_=c2_spread[:])
+        for b in range(ROW_BLOCKS):
+            sum_squared_features(b)
 
-        for v in range(VIEWS):
-            project(1, v)
-        multiply_by_centers(0)
-
-        sum_squared_features(1)
-        quantise_features(1)
-
-        multiply_by_centers(1)
+        for b in range(ROW_BLOCKS):
+            multiply_by_centers(b)
 
         for b in range(ROW_BLOCKS):
             partial = stage.tile([P, NCLASS], F32)

@@ -15,27 +15,29 @@ P = 128
 PACK = 4
 HALVES = 2
 K_PASS = P * PACK
+PSUM_BANKS = 8
 
 BATCH, IN_F, FEAT, NCLASS = 256, 1024, 128, 256
 VIEWS = 4
+WEIGHTS = 2
 JOINED = VIEWS * FEAT
 PASSES = IN_F // K_PASS
 ROW_BLOCKS = BATCH // P
 CLASS_BLOCKS = NCLASS // P
 GAMMA = 0.1
-PSUM_BANKS = 8
+SQRT_FLOOR = 2.0**-116
 
 FLOPS = 2 * BATCH * IN_F * FEAT * VIEWS + 2 * BATCH * JOINED * NCLASS
 
 
-def quantise_rows(nc, copy_out, psum, stage_pool, rows_sb, ident_f32, codes, scales):
+def quantise_rows(nc, copy_out, psum, stage, rows_sb, ident_f32, codes, scales):
     pairs = rows_sb[:].bitcast(F32)
     flipped = psum.tile([P, PASSES, HALVES, P], F32, tag="bank")
     for g in range(PASSES):
         for u in range(HALVES):
             first = (g * HALVES + u) * P
             nc.tensor.transpose(flipped[:, g, u, :], pairs[:, first : first + P], ident_f32[:])
-    grouped = stage_pool.tile([P, PASSES * P * PACK], BF16, align_bytes=64, tag="grouped")
+    grouped = stage.tile([P, PASSES * P * PACK], BF16, align_bytes=64)
     copy_out(
         out=grouped[:].bitcast(F32).rearrange("p (g r u) -> p g r u", g=PASSES, u=HALVES),
         in_=flipped[:].rearrange("p g u r -> p g r u"),
@@ -51,23 +53,22 @@ def tile_qccpn_pa_s_kernel(tc, x, x_90, x_180, x_270, W_f, b_f, W_r, b_r, center
     with ExitStack() as stack:
         stack.enter_context(tc.manual_schedule())
         const = stack.enter_context(tc.tile_pool(name="const", bufs=1))
-        rows_pool = stack.enter_context(tc.tile_pool(name="rows", bufs=VIEWS * ROW_BLOCKS))
-        stage = stack.enter_context(tc.tile_pool(name="stage", bufs=3))
-        per_view = stack.enter_context(tc.tile_pool(name="per_view", bufs=VIEWS * ROW_BLOCKS))
+        per_view = stack.enter_context(tc.tile_pool(name="per_view", bufs=ROW_BLOCKS * VIEWS))
         per_block = stack.enter_context(tc.tile_pool(name="per_block", bufs=ROW_BLOCKS))
+        stage = stack.enter_context(tc.tile_pool(name="stage", bufs=3))
         psum = stack.enter_context(tc.psum_pool(name="psum", bufs=PSUM_BANKS))
 
-        bias_bf = [const.tile([FEAT, 1], BF16, name="bias_bf%d" % w) for w in range(2)]
+        bias_bf = [const.tile([FEAT, 1], BF16, name="bias_bf%d" % w) for w in range(WEIGHTS)]
         with nc.allow_non_contiguous_dma(reason="a bias of 128 values, one to a partition"):
             for w, b_dram in enumerate([b_f, b_r]):
                 nc.scalar.dma_start(out=bias_bf[w][:], in_=b_dram.rearrange("(f o) -> f o", o=1))
 
-        w_rows = [const.tile([FEAT, IN_F], BF16, name="w_rows%d" % w) for w in range(2)]
+        cen_rows = const.tile([P, CLASS_BLOCKS, JOINED], BF16)
+        w_rows = [const.tile([FEAT, IN_F], BF16, name="w_rows%d" % w) for w in range(WEIGHTS)]
         x_rows = {}
         for b in range(ROW_BLOCKS):
             for v in range(VIEWS):
-                x_rows[(b, v)] = rows_pool.tile([P, IN_F], BF16, name="x_rows", tag="x_rows")
-        cen_rows = const.tile([P, CLASS_BLOCKS, JOINED], BF16)
+                x_rows[(b, v)] = per_view.tile([P, IN_F], BF16, name="x_rows")
 
         def load_x(b, v):
             nc.sync.dma_start(out=x_rows[(b, v)][:], in_=views[v][b * P : (b + 1) * P, :])
@@ -91,9 +92,10 @@ def tile_qccpn_pa_s_kernel(tc, x, x_90, x_180, x_270, W_f, b_f, W_r, b_r, center
         ident_bf = const.tile([P, P], BF16)
         nc.vector.tensor_copy(out=ident_bf[:], in_=ident_f32[:])
 
-        w_codes = [const.tile([P, PASSES * FEAT], U32, align_bytes=64, name="w_codes%d" % w) for w in range(2)]
-        w_scales = [const.tile([P, PASSES * FEAT], U8, align_bytes=64, name="w_scales%d" % w) for w in range(2)]
-        x_codes, x_scales, feat, feat_grouped, f2, feat_codes, feat_scales, dot, root = {}, {}, {}, {}, {}, {}, {}, {}, {}
+        w_codes = [const.tile([P, PASSES * FEAT], U32, align_bytes=64, name="w_codes%d" % w) for w in range(WEIGHTS)]
+        w_scales = [const.tile([P, PASSES * FEAT], U8, align_bytes=64, name="w_scales%d" % w) for w in range(WEIGHTS)]
+        x_codes, x_scales, feat = {}, {}, {}
+        feat_grouped, feat_codes, feat_scales, f2, dot, partial, root = {}, {}, {}, {}, {}, {}, {}
 
         banks_emptied = []
 
@@ -163,8 +165,6 @@ def tile_qccpn_pa_s_kernel(tc, x, x_90, x_180, x_270, W_f, b_f, W_r, b_r, center
                 stop=True,
             )
 
-        for b in range(ROW_BLOCKS):
-            feat_grouped[b] = per_block.tile([P, P, VIEWS], BF16, align_bytes=64, name="feat_grouped")
         cen_flipped = psum.tile([P, CLASS_BLOCKS, VIEWS, P], BF16, tag="bank")
         for cb in range(CLASS_BLOCKS):
             for v in range(VIEWS):
@@ -195,11 +195,12 @@ def tile_qccpn_pa_s_kernel(tc, x, x_90, x_180, x_270, W_f, b_f, W_r, b_r, center
         for v in range(VIEWS):
             quantise_view(1, v)
 
-        bias = [const.tile([FEAT, 1], F32, name="bias%d" % w) for w in range(2)]
-        for w in range(2):
+        bias = [const.tile([FEAT, 1], F32, name="bias%d" % w) for w in range(WEIGHTS)]
+        for w in range(WEIGHTS):
             nc.vector.tensor_copy(out=bias[w][:], in_=bias_bf[w][:])
 
         for b in range(ROW_BLOCKS):
+            feat_grouped[b] = per_block.tile([P, P, VIEWS], BF16, align_bytes=64, name="feat_grouped")
             for v in range(VIEWS):
                 project(b, v)
             quantise_features(b)
@@ -216,13 +217,14 @@ def tile_qccpn_pa_s_kernel(tc, x, x_90, x_180, x_270, W_f, b_f, W_r, b_r, center
             multiply_by_centers(b)
 
         for b in range(ROW_BLOCKS):
-            partial = stage.tile([P, NCLASS], F32)
+            partial[b] = per_block.tile([P, NCLASS], F32, name="partial")
             nc.vector.scalar_tensor_tensor(
-                out=partial[:], in0=dot[b][:], scalar=-2.0, in1=c2_all[:], op0=ALU.mult, op1=ALU.add
+                out=partial[b][:], in0=dot[b][:], scalar=-2.0, in1=c2_all[:], op0=ALU.mult, op1=ALU.add
             )
+        for b in range(ROW_BLOCKS):
             d2 = stage.tile([P, NCLASS], F32)
             nc.vector.tensor_scalar(
-                out=d2[:], in0=partial[:], scalar1=f2[b][:, 0:1], scalar2=0.0, op0=ALU.add, op1=ALU.max
+                out=d2[:], in0=partial[b][:], scalar1=f2[b][:, 0:1], scalar2=SQRT_FLOOR, op0=ALU.add, op1=ALU.max
             )
             root[b] = per_block.tile([P, NCLASS], F32, name="root")
             nc.scalar.activation(out=root[b][:], in_=d2[:], func=ACT.Sqrt)

@@ -30,7 +30,7 @@ SQRT_FLOOR = 2.0**-116
 FLOPS = 2 * BATCH * IN_F * FEAT * VIEWS + 2 * BATCH * JOINED * NCLASS
 
 
-def quantise_rows(nc, copy_out, psum, stage, rows_sb, ident_f32, codes, scales):
+def regroup_rows(nc, copy_out, psum, stage, rows_sb, ident_f32):
     pairs = rows_sb[:].bitcast(F32)
     flipped = psum.tile([P, PASSES, HALVES, P], F32, tag="bank")
     for g in range(PASSES):
@@ -42,7 +42,7 @@ def quantise_rows(nc, copy_out, psum, stage, rows_sb, ident_f32, codes, scales):
         out=grouped[:].bitcast(F32).rearrange("p (g r u) -> p g r u", g=PASSES, u=HALVES),
         in_=flipped[:].rearrange("p g u r -> p g r u"),
     )
-    nc.vector.quantize_mx(out=codes.bitcast(FP8X4), scales=scales, in_=grouped[:])
+    return grouped
 
 
 def tile_qccpn_pa_s_kernel(tc, x, x_90, x_180, x_270, W_f, b_f, W_r, b_r, centers, out):
@@ -58,10 +58,10 @@ def tile_qccpn_pa_s_kernel(tc, x, x_90, x_180, x_270, W_f, b_f, W_r, b_r, center
         stage = stack.enter_context(tc.tile_pool(name="stage", bufs=3))
         psum = stack.enter_context(tc.psum_pool(name="psum", bufs=PSUM_BANKS))
 
-        bias_bf = [const.tile([FEAT, 1], BF16, name="bias_bf%d" % w) for w in range(WEIGHTS)]
+        bias = [const.tile([FEAT, 1], BF16, name="bias%d" % w) for w in range(WEIGHTS)]
         with nc.allow_non_contiguous_dma(reason="a bias of 128 values, one to a partition"):
             for w, b_dram in enumerate([b_f, b_r]):
-                nc.scalar.dma_start(out=bias_bf[w][:], in_=b_dram.rearrange("(f o) -> f o", o=1))
+                nc.scalar.dma_start(out=bias[w][:], in_=b_dram.rearrange("(f o) -> f o", o=1))
 
         cen_rows = const.tile([P, CLASS_BLOCKS, JOINED], BF16)
         w_rows = [const.tile([FEAT, IN_F], BF16, name="w_rows%d" % w) for w in range(WEIGHTS)]
@@ -106,14 +106,26 @@ def tile_qccpn_pa_s_kernel(tc, x, x_90, x_180, x_270, W_f, b_f, W_r, b_r, center
                 nc.scalar.copy(out=out, in_=in_)
             banks_emptied.append(1)
 
+        waiting = [None]
+
+        def quantise_waiting():
+            if waiting[0] is not None:
+                codes, scales, grouped = waiting[0]
+                nc.vector.quantize_mx(out=codes[:].bitcast(FP8X4), scales=scales[:], in_=grouped[:])
+            waiting[0] = None
+
+        def quantise_later(codes, scales, grouped):
+            quantise_waiting()
+            waiting[0] = (codes, scales, grouped)
+
         def quantise_weight(w):
-            quantise_rows(nc, copy_out, psum, stage, w_rows[w], ident_f32, w_codes[w][:], w_scales[w][:])
+            quantise_later(w_codes[w], w_scales[w], regroup_rows(nc, copy_out, psum, stage, w_rows[w], ident_f32))
 
         def quantise_view(b, v):
             x_codes[(b, v)] = per_view.tile([P, PASSES * P], U32, align_bytes=64, name="x_codes")
             x_scales[(b, v)] = per_view.tile([P, PASSES * P], U8, align_bytes=64, name="x_scales")
-            quantise_rows(
-                nc, copy_out, psum, stage, x_rows[(b, v)], ident_f32, x_codes[(b, v)][:], x_scales[(b, v)][:]
+            quantise_later(
+                x_codes[(b, v)], x_scales[(b, v)], regroup_rows(nc, copy_out, psum, stage, x_rows[(b, v)], ident_f32)
             )
 
         def project(b, v):
@@ -176,7 +188,7 @@ def tile_qccpn_pa_s_kernel(tc, x, x_90, x_180, x_270, W_f, b_f, W_r, b_r, center
         )
         cen_codes = const.tile([P, NCLASS], U32, align_bytes=64)
         cen_scales = const.tile([P, NCLASS], U8, align_bytes=64)
-        nc.vector.quantize_mx(out=cen_codes[:].bitcast(FP8X4), scales=cen_scales[:], in_=cen_grouped[:])
+        quantise_later(cen_codes, cen_scales, cen_grouped)
 
         c2_col = const.tile([P, CLASS_BLOCKS], F32)
         cen_squares = const.tile([P, CLASS_BLOCKS, JOINED], F32)
@@ -194,10 +206,7 @@ def tile_qccpn_pa_s_kernel(tc, x, x_90, x_180, x_270, W_f, b_f, W_r, b_r, center
             quantise_view(0, v)
         for v in range(VIEWS):
             quantise_view(1, v)
-
-        bias = [const.tile([FEAT, 1], F32, name="bias%d" % w) for w in range(WEIGHTS)]
-        for w in range(WEIGHTS):
-            nc.vector.tensor_copy(out=bias[w][:], in_=bias_bf[w][:])
+        quantise_waiting()
 
         for b in range(ROW_BLOCKS):
             feat_grouped[b] = per_block.tile([P, P, VIEWS], BF16, align_bytes=64, name="feat_grouped")

@@ -94,8 +94,8 @@ def tile_qccpn_pa_s_kernel(tc, x, x_90, x_180, x_270, W_f, b_f, W_r, b_r, center
 
         w_codes = [const.tile([P, PASSES * FEAT], U32, align_bytes=64, name="w_codes%d" % w) for w in range(WEIGHTS)]
         w_scales = [const.tile([P, PASSES * FEAT], U8, align_bytes=64, name="w_scales%d" % w) for w in range(WEIGHTS)]
-        x_codes, x_scales, feat = {}, {}, {}
-        feat_grouped, feat_codes, feat_scales, f2, dot, partial, root = {}, {}, {}, {}, {}, {}, {}
+        x_codes, x_scales = {}, {}
+        feat, feat_grouped, feat_codes, feat_scales, f2, dot, partial, root = {}, {}, {}, {}, {}, {}, {}, {}
 
         banks_emptied = []
 
@@ -142,11 +142,11 @@ def tile_qccpn_pa_s_kernel(tc, x, x_90, x_180, x_270, W_f, b_f, W_r, b_r, center
                     start=(g == 0),
                     stop=(g == PASSES - 1),
                 )
-            feat[(b, v)] = per_view.tile([FEAT, P], F32, name="feat")
-            nc.scalar.activation(out=feat[(b, v)][:], in_=feat_t[:], func=ACT.Relu, bias=bias[w][:, 0:1])
-            nc.vector.tensor_copy(out=feat_grouped[b][:, :, v], in_=feat[(b, v)][:])
+            nc.scalar.activation(out=feat[b][:, v, :], in_=feat_t[:], func=ACT.Relu, bias=bias[w][:, 0:1])
 
         def quantise_features(b):
+            feat_grouped[b] = per_block.tile([P, P, VIEWS], BF16, align_bytes=64, name="feat_grouped")
+            nc.vector.tensor_copy(out=feat_grouped[b][:], in_=feat[b][:].rearrange("p v i -> p i v"))
             feat_codes[b] = per_block.tile([P, P], U32, align_bytes=64, name="feat_codes")
             feat_scales[b] = per_block.tile([P, P], U8, align_bytes=64, name="feat_scales")
             nc.vector.quantize_mx(
@@ -158,7 +158,7 @@ def tile_qccpn_pa_s_kernel(tc, x, x_90, x_180, x_270, W_f, b_f, W_r, b_r, center
         def sum_squared_features(b):
             feat_rows = psum.tile([P, VIEWS, FEAT], F32, tag="bank")
             for v in range(VIEWS):
-                nc.tensor.transpose(feat_rows[:, v, :], feat[(b, v)][:], ident_f32[:])
+                nc.tensor.transpose(feat_rows[:, v, :], feat[b][:, v, :], ident_f32[:])
             f2[b] = per_block.tile([P, 1], F32, name="f2")
             feat_squares = stage.tile([P, JOINED], F32)
             nc.scalar.activation(
@@ -209,7 +209,7 @@ def tile_qccpn_pa_s_kernel(tc, x, x_90, x_180, x_270, W_f, b_f, W_r, b_r, center
         quantise_waiting()
 
         for b in range(ROW_BLOCKS):
-            feat_grouped[b] = per_block.tile([P, P, VIEWS], BF16, align_bytes=64, name="feat_grouped")
+            feat[b] = per_block.tile([FEAT, VIEWS, P], F32, name="feat")
             for v in range(VIEWS):
                 project(b, v)
             quantise_features(b)

@@ -97,14 +97,7 @@ def tile_qccpn_pa_s_kernel(tc, x, x_90, x_180, x_270, W_f, b_f, W_r, b_r, center
         x_codes, x_scales = {}, {}
         feat, feat_grouped, feat_codes, feat_scales, f2, dot, partial, root = {}, {}, {}, {}, {}, {}, {}, {}
 
-        banks_emptied = []
-
-        def copy_out(out, in_):
-            if len(banks_emptied) % 3 == 0:
-                nc.vector.tensor_copy(out=out, in_=in_)
-            else:
-                nc.scalar.copy(out=out, in_=in_)
-            banks_emptied.append(1)
+        on_scalar, on_vector = nc.scalar.copy, nc.vector.tensor_copy
 
         waiting = [None]
 
@@ -118,35 +111,51 @@ def tile_qccpn_pa_s_kernel(tc, x, x_90, x_180, x_270, W_f, b_f, W_r, b_r, center
             quantise_waiting()
             waiting[0] = (codes, scales, grouped)
 
-        def quantise_weight(w):
+        def quantise_weight(w, copy_out):
             quantise_later(w_codes[w], w_scales[w], regroup_rows(nc, copy_out, psum, stage, w_rows[w], ident_f32))
 
-        def quantise_view(b, v):
+        def quantise_view(b, v, copy_out):
             x_codes[(b, v)] = per_view.tile([P, PASSES * P], U32, align_bytes=64, name="x_codes")
             x_scales[(b, v)] = per_view.tile([P, PASSES * P], U8, align_bytes=64, name="x_scales")
             quantise_later(
                 x_codes[(b, v)], x_scales[(b, v)], regroup_rows(nc, copy_out, psum, stage, x_rows[(b, v)], ident_f32)
             )
 
-        def project(b, v):
-            w = weight_of_view[v]
-            feat_t = psum.tile([FEAT, P], F32, tag="bank")
-            for g in range(PASSES):
-                cols = slice(g * P, (g + 1) * P)
-                nc.tensor.matmul_mx(
-                    out=feat_t[:],
-                    lhsT=w_codes[w][:, cols].bitcast(FP8X4),
-                    lhsT_scale=w_scales[w][:, cols],
-                    rhs=x_codes[(b, v)][:, cols].bitcast(FP8X4),
-                    rhs_scale=x_scales[(b, v)][:, cols],
-                    start=(g == 0),
-                    stop=(g == PASSES - 1),
-                )
-            nc.scalar.activation(out=feat[b][:, v, :], in_=feat_t[:], func=ACT.Relu, bias=bias[w][:, 0:1])
+        feat_t = {}
 
-        def quantise_features(b):
+        def project(b, views_of_bank):
+            bank = psum.tile([FEAT, len(views_of_bank), P], F32, name="feat_t", tag="bank")
+            for n, v in enumerate(views_of_bank):
+                w = weight_of_view[v]
+                for g in range(PASSES):
+                    cols = slice(g * P, (g + 1) * P)
+                    nc.tensor.matmul_mx(
+                        out=bank[:, n, :],
+                        lhsT=w_codes[w][:, cols].bitcast(FP8X4),
+                        lhsT_scale=w_scales[w][:, cols],
+                        rhs=x_codes[(b, v)][:, cols].bitcast(FP8X4),
+                        rhs_scale=x_scales[(b, v)][:, cols],
+                        start=(g == 0),
+                        stop=(g == PASSES - 1),
+                    )
+            feat_t[(b, views_of_bank[0])] = bank
+
+        def relu(b, views_of_bank, on_engine="scalar"):
+            v0 = views_of_bank[0]
+            bias_col = bias[weight_of_view[v0]][:, 0:1]
+            feat_v = feat[b][:, v0 : v0 + len(views_of_bank), :]
+            if on_engine == "vector":
+                nc.vector.tensor_scalar(
+                    out=feat_v, in0=feat_t[(b, v0)][:], scalar1=bias_col, scalar2=0.0, op0=ALU.add, op1=ALU.max
+                )
+            else:
+                nc.scalar.activation(out=feat_v, in_=feat_t[(b, v0)][:], func=ACT.Relu, bias=bias_col)
+
+        def round_features(b):
             feat_grouped[b] = per_block.tile([P, P, VIEWS], BF16, align_bytes=64, name="feat_grouped")
             nc.vector.tensor_copy(out=feat_grouped[b][:], in_=feat[b][:].rearrange("p v i -> p i v"))
+
+        def quantise_features(b):
             feat_codes[b] = per_block.tile([P, P], U32, align_bytes=64, name="feat_codes")
             feat_scales[b] = per_block.tile([P, P], U8, align_bytes=64, name="feat_scales")
             nc.vector.quantize_mx(
@@ -177,15 +186,34 @@ def tile_qccpn_pa_s_kernel(tc, x, x_90, x_180, x_270, W_f, b_f, W_r, b_r, center
                 stop=True,
             )
 
-        cen_flipped = psum.tile([P, CLASS_BLOCKS, VIEWS, P], BF16, tag="bank")
-        for cb in range(CLASS_BLOCKS):
-            for v in range(VIEWS):
-                nc.tensor.transpose(cen_flipped[:, cb, v, :], cen_rows[:, cb, v * P : (v + 1) * P], ident_bf[:])
+        def combine(b):
+            partial[b] = per_block.tile([P, NCLASS], F32, name="partial")
+            nc.vector.scalar_tensor_tensor(
+                out=partial[b][:], in0=dot[b][:], scalar=-2.0, in1=c2_all[:], op0=ALU.mult, op1=ALU.add
+            )
+
+        def root_of(b):
+            d2 = stage.tile([P, NCLASS], F32)
+            nc.vector.tensor_scalar(
+                out=d2[:], in0=partial[b][:], scalar1=f2[b][:, 0:1], scalar2=SQRT_FLOOR, op0=ALU.add, op1=ALU.max
+            )
+            root[b] = per_block.tile([P, NCLASS], F32, name="root")
+            nc.scalar.activation(out=root[b][:], in_=d2[:], func=ACT.Sqrt)
+
+        def store(b):
+            score = stage.tile([P, NCLASS], F32)
+            nc.vector.tensor_scalar_mul(out=score[:], in0=root[b][:], scalar1=-GAMMA)
+            nc.sync.dma_start(out=out[b * P : (b + 1) * P, :], in_=score[:])
+
         cen_grouped = const.tile([P, NCLASS * PACK], BF16, align_bytes=64)
-        copy_out(
-            out=cen_grouped[:].rearrange("p (cb c v) -> p cb c v", cb=CLASS_BLOCKS, v=VIEWS),
-            in_=cen_flipped[:].rearrange("p cb v c -> p cb c v"),
-        )
+        for cb in range(CLASS_BLOCKS):
+            cen_flipped = psum.tile([P, VIEWS, P], BF16, tag="bank")
+            for v in range(VIEWS):
+                nc.tensor.transpose(cen_flipped[:, v, :], cen_rows[:, cb, v * P : (v + 1) * P], ident_bf[:])
+            nc.vector.tensor_copy(
+                out=cen_grouped[:, cb * P * PACK : (cb + 1) * P * PACK].rearrange("p (c v) -> p c v", v=VIEWS),
+                in_=cen_flipped[:].rearrange("p v c -> p c v"),
+            )
         cen_codes = const.tile([P, NCLASS], U32, align_bytes=64)
         cen_scales = const.tile([P, NCLASS], U8, align_bytes=64)
         quantise_later(cen_codes, cen_scales, cen_grouped)
@@ -196,48 +224,43 @@ def tile_qccpn_pa_s_kernel(tc, x, x_90, x_180, x_270, W_f, b_f, W_r, b_r, center
             nc.scalar.activation(
                 out=cen_squares[:, cb, :], in_=cen_rows[:, cb, :], func=ACT.Square, accum_out=c2_col[:, cb : cb + 1]
             )
-        c2_repeated = const.tile([P, CLASS_BLOCKS, P], F32)
-        nc.vector.tensor_copy(out=c2_repeated[:], in_=c2_col[:].unsqueeze(2).to_broadcast([P, CLASS_BLOCKS, P]))
 
-        quantise_weight(0)
-        quantise_view(0, 0)
-        quantise_weight(1)
-        for v in range(1, VIEWS):
-            quantise_view(0, v)
-        for v in range(VIEWS):
-            quantise_view(1, v)
-        quantise_waiting()
-
-        for b in range(ROW_BLOCKS):
-            feat[b] = per_block.tile([FEAT, VIEWS, P], F32, name="feat")
-            for v in range(VIEWS):
-                project(b, v)
-            quantise_features(b)
-
+        quantise_weight(0, on_scalar)
+        quantise_view(0, 0, on_vector)
+        quantise_weight(1, on_scalar)
         c2_spread = psum.tile([P, NCLASS], F32, tag="bank")
         for cb in range(CLASS_BLOCKS):
-            nc.tensor.transpose(c2_spread[:, cb * P : (cb + 1) * P], c2_repeated[:, cb, :], ident_f32[:])
+            nc.tensor.transpose(
+                c2_spread[:, cb * P : (cb + 1) * P], c2_col[:, cb : cb + 1].to_broadcast([P, P]), ident_f32[:]
+            )
+        quantise_view(0, 1, on_scalar)
         c2_all = const.tile([P, NCLASS], F32)
         nc.vector.tensor_copy(out=c2_all[:], in_=c2_spread[:])
+        quantise_view(0, 2, on_scalar)
+        quantise_view(0, 3, on_vector)
+        for v in range(VIEWS):
+            quantise_view(1, v, on_scalar)
+        for b in range(ROW_BLOCKS):
+            feat[b] = per_block.tile([FEAT, VIEWS, P], F32, name="feat")
+        project(0, [0])
+        project(0, [1, 2, 3])
+        relu(0, [0])
+        relu(0, [1, 2, 3])
+        quantise_waiting()
+        for v in range(VIEWS):
+            project(1, [v])
+            relu(1, [v], "vector" if v < 2 else "scalar")
+        for b in range(ROW_BLOCKS):
+            round_features(b)
+        for b in range(ROW_BLOCKS):
+            quantise_features(b)
         for b in range(ROW_BLOCKS):
             sum_squared_features(b)
-
         for b in range(ROW_BLOCKS):
             multiply_by_centers(b)
-
         for b in range(ROW_BLOCKS):
-            partial[b] = per_block.tile([P, NCLASS], F32, name="partial")
-            nc.vector.scalar_tensor_tensor(
-                out=partial[b][:], in0=dot[b][:], scalar=-2.0, in1=c2_all[:], op0=ALU.mult, op1=ALU.add
-            )
+            combine(b)
         for b in range(ROW_BLOCKS):
-            d2 = stage.tile([P, NCLASS], F32)
-            nc.vector.tensor_scalar(
-                out=d2[:], in0=partial[b][:], scalar1=f2[b][:, 0:1], scalar2=SQRT_FLOOR, op0=ALU.add, op1=ALU.max
-            )
-            root[b] = per_block.tile([P, NCLASS], F32, name="root")
-            nc.scalar.activation(out=root[b][:], in_=d2[:], func=ACT.Sqrt)
+            root_of(b)
         for b in range(ROW_BLOCKS):
-            score = stage.tile([P, NCLASS], F32)
-            nc.vector.tensor_scalar_mul(out=score[:], in0=root[b][:], scalar1=-GAMMA)
-            nc.sync.dma_start(out=out[b * P : (b + 1) * P, :], in_=score[:])
+            store(b)

@@ -25,6 +25,7 @@ PASSES = IN_F // K_PASS
 ROW_BLOCKS = BATCH // P
 CLASS_BLOCKS = NCLASS // P
 GAMMA = 0.1
+HEAD_MATMULS = 3
 SQRT_FLOOR = 2.0**-116
 
 FLOPS = 2 * BATCH * IN_F * FEAT * VIEWS + 2 * BATCH * JOINED * NCLASS
@@ -56,7 +57,8 @@ def tile_qccpn_pa_s_kernel(tc, x, x_90, x_180, x_270, W_f, b_f, W_r, b_r, center
         per_view = stack.enter_context(tc.tile_pool(name="per_view", bufs=ROW_BLOCKS * VIEWS))
         per_block = stack.enter_context(tc.tile_pool(name="per_block", bufs=ROW_BLOCKS))
         stage = stack.enter_context(tc.tile_pool(name="stage", bufs=3))
-        psum = stack.enter_context(tc.psum_pool(name="psum", bufs=PSUM_BANKS))
+        psum = stack.enter_context(tc.psum_pool(name="psum", bufs=PSUM_BANKS - 1))
+        unread_pool = stack.enter_context(tc.psum_pool(name="unread_pool", bufs=1))
 
         bias = [const.tile([FEAT, 1], BF16, name="bias%d" % w) for w in range(WEIGHTS)]
         with nc.allow_non_contiguous_dma(reason="a bias of 128 values, one to a partition"):
@@ -83,6 +85,15 @@ def tile_qccpn_pa_s_kernel(tc, x, x_90, x_180, x_270, W_f, b_f, W_r, b_r, center
         for v in range(VIEWS):
             load_x(1, v)
 
+        zeros = const.tile([P, P], F32)
+        nc.vector.memset(zeros[:], 0.0)
+        unread = unread_pool.tile([P, P], F32)
+
+        def keep_busy(columns):
+            nc.tensor.matmul(out=unread[:, 0:columns], lhsT=zeros[:], rhs=zeros[:, 0:columns], start=True, stop=True)
+
+        for step in range(HEAD_MATMULS):
+            keep_busy(P)
         one = const.tile([P, 1], F32)
         nc.vector.memset(one[:], 1.0)
         one_root = const.tile([P, 1], F32)
@@ -112,9 +123,12 @@ def tile_qccpn_pa_s_kernel(tc, x, x_90, x_180, x_270, W_f, b_f, W_r, b_r, center
             waiting[0] = (codes, scales, grouped)
 
         def quantise_weight(w, copy_out):
+            keep_busy(P // 2)
             quantise_later(w_codes[w], w_scales[w], regroup_rows(nc, copy_out, psum, stage, w_rows[w], ident_f32))
 
         def quantise_view(b, v, copy_out):
+            if (b, v) != (0, 0):
+                keep_busy(P // 2)
             x_codes[(b, v)] = per_view.tile([P, PASSES * P], U32, align_bytes=64, name="x_codes")
             x_scales[(b, v)] = per_view.tile([P, PASSES * P], U8, align_bytes=64, name="x_scales")
             quantise_later(

@@ -25,15 +25,18 @@ PASSES = IN_F // K_PASS
 ROW_BLOCKS = BATCH // P
 CLASS_BLOCKS = NCLASS // P
 GAMMA = 0.1
+KEEP_BUSY = [(0, 2), (1, 0), (1, 2)]
 HEAD_MATMULS = 3
 SQRT_FLOOR = 2.0**-116
 
 FLOPS = 2 * BATCH * IN_F * FEAT * VIEWS + 2 * BATCH * JOINED * NCLASS
 
 
-def regroup_rows(nc, copy_out, psum, stage, rows_sb, ident_f32):
+def regroup_rows(nc, copy_out, psum, stage, rows_sb, ident_f32, zeros=None):
     pairs = rows_sb[:].bitcast(F32)
     flipped = psum.tile([P, PASSES, HALVES, P], F32, tag="bank")
+    if zeros is not None:
+        nc.tensor.matmul(out=flipped[:, 0, 0, :], lhsT=zeros[:], rhs=zeros[:], start=True, stop=True)
     for g in range(PASSES):
         for u in range(HALVES):
             first = (g * HALVES + u) * P
@@ -57,8 +60,7 @@ def tile_qccpn_pa_s_kernel(tc, x, x_90, x_180, x_270, W_f, b_f, W_r, b_r, center
         per_view = stack.enter_context(tc.tile_pool(name="per_view", bufs=ROW_BLOCKS * VIEWS))
         per_block = stack.enter_context(tc.tile_pool(name="per_block", bufs=ROW_BLOCKS))
         stage = stack.enter_context(tc.tile_pool(name="stage", bufs=3))
-        psum = stack.enter_context(tc.psum_pool(name="psum", bufs=PSUM_BANKS - 1))
-        unread_pool = stack.enter_context(tc.psum_pool(name="unread_pool", bufs=1))
+        psum = stack.enter_context(tc.psum_pool(name="psum", bufs=PSUM_BANKS))
 
         bias = [const.tile([FEAT, 1], BF16, name="bias%d" % w) for w in range(WEIGHTS)]
         with nc.allow_non_contiguous_dma(reason="a bias of 128 values, one to a partition"):
@@ -87,13 +89,9 @@ def tile_qccpn_pa_s_kernel(tc, x, x_90, x_180, x_270, W_f, b_f, W_r, b_r, center
 
         zeros = const.tile([P, P], F32)
         nc.vector.memset(zeros[:], 0.0)
-        unread = unread_pool.tile([P, P], F32)
-
-        def keep_busy(columns):
-            nc.tensor.matmul(out=unread[:, 0:columns], lhsT=zeros[:], rhs=zeros[:, 0:columns], start=True, stop=True)
-
+        unread = psum.tile([P, P], F32, tag="bank")
         for step in range(HEAD_MATMULS):
-            keep_busy(P)
+            nc.tensor.matmul(out=unread[:], lhsT=zeros[:], rhs=zeros[:], start=True, stop=True)
         one = const.tile([P, 1], F32)
         nc.vector.memset(one[:], 1.0)
         one_root = const.tile([P, 1], F32)
@@ -123,16 +121,15 @@ def tile_qccpn_pa_s_kernel(tc, x, x_90, x_180, x_270, W_f, b_f, W_r, b_r, center
             waiting[0] = (codes, scales, grouped)
 
         def quantise_weight(w, copy_out):
-            keep_busy(P // 2)
-            quantise_later(w_codes[w], w_scales[w], regroup_rows(nc, copy_out, psum, stage, w_rows[w], ident_f32))
+            quantise_later(w_codes[w], w_scales[w], regroup_rows(nc, copy_out, psum, stage, w_rows[w], ident_f32, zeros if w == 1 else None))
 
         def quantise_view(b, v, copy_out):
-            if (b, v) != (0, 0):
-                keep_busy(P // 2)
             x_codes[(b, v)] = per_view.tile([P, PASSES * P], U32, align_bytes=64, name="x_codes")
             x_scales[(b, v)] = per_view.tile([P, PASSES * P], U8, align_bytes=64, name="x_scales")
             quantise_later(
-                x_codes[(b, v)], x_scales[(b, v)], regroup_rows(nc, copy_out, psum, stage, x_rows[(b, v)], ident_f32)
+                x_codes[(b, v)],
+                x_scales[(b, v)],
+                regroup_rows(nc, copy_out, psum, stage, x_rows[(b, v)], ident_f32, zeros if (b, v) in KEEP_BUSY else None),
             )
 
         feat_t = {}

from contextlib import ExitStack

import concourse.mybir as mybir
from concourse.masks import make_identity

F32 = mybir.dt.float32
BF16 = mybir.dt.bfloat16
U32 = mybir.dt.uint32
U8 = mybir.dt.uint8
FP8X4 = mybir.dt.float8_e4m3fn_x4
ALU = mybir.AluOpType
ACT = mybir.ActivationFunctionType

P = 128
PACK = 4
HALVES = 2
K_PASS = P * PACK
PSUM_BANKS = 8

BATCH, IN_F, FEAT, NCLASS = 256, 1024, 128, 256
VIEWS = 4
WEIGHTS = 2
JOINED = VIEWS * FEAT
PASSES = IN_F // K_PASS
ROW_BLOCKS = BATCH // P
CLASS_BLOCKS = NCLASS // P
GAMMA = 0.1
KEEP_BUSY = [(0, 2), (1, 0), (1, 2)]
HEAD_MATMULS = 3
SQRT_FLOOR = 2.0**-116

FLOPS = 2 * BATCH * IN_F * FEAT * VIEWS + 2 * BATCH * JOINED * NCLASS


def regroup_rows(nc, copy_out, psum, stage, rows_sb, ident_f32, zeros=None):
    pairs = rows_sb[:].bitcast(F32)
    flipped = psum.tile([P, PASSES, HALVES, P], F32, tag="bank")
    if zeros is not None:
        nc.tensor.matmul(out=flipped[:, 0, 0, :], lhsT=zeros[:], rhs=zeros[:], start=True, stop=True)
    for g in range(PASSES):
        for u in range(HALVES):
            first = (g * HALVES + u) * P
            nc.tensor.transpose(flipped[:, g, u, :], pairs[:, first : first + P], ident_f32[:])
    grouped = stage.tile([P, PASSES * P * PACK], BF16, align_bytes=64)
    copy_out(
        out=grouped[:].bitcast(F32).rearrange("p (g r u) -> p g r u", g=PASSES, u=HALVES),
        in_=flipped[:].rearrange("p g u r -> p g r u"),
    )
    return grouped


def tile_qccpn_pa_s_kernel(tc, x, x_90, x_180, x_270, W_f, b_f, W_r, b_r, centers, out):
    nc = tc.nc
    views = [x, x_90, x_180, x_270]
    weight_of_view = [0, 1, 1, 1]

    with ExitStack() as stack:
        stack.enter_context(tc.manual_schedule())
        const = stack.enter_context(tc.tile_pool(name="const", bufs=1))
        per_view = stack.enter_context(tc.tile_pool(name="per_view", bufs=ROW_BLOCKS * VIEWS))
        per_block = stack.enter_context(tc.tile_pool(name="per_block", bufs=ROW_BLOCKS))
        stage = stack.enter_context(tc.tile_pool(name="stage", bufs=3))
        psum = stack.enter_context(tc.psum_pool(name="psum", bufs=PSUM_BANKS))

        bias = [const.tile([FEAT, 1], BF16, name="bias%d" % w) for w in range(WEIGHTS)]
        with nc.allow_non_contiguous_dma(reason="a bias of 128 values, one to a partition"):
            for w, b_dram in enumerate([b_f, b_r]):
                nc.scalar.dma_start(out=bias[w][:], in_=b_dram.rearrange("(f o) -> f o", o=1))

        cen_rows = const.tile([P, CLASS_BLOCKS, JOINED], BF16)
        w_rows = [const.tile([FEAT, IN_F], BF16, name="w_rows%d" % w) for w in range(WEIGHTS)]
        x_rows = {}
        for b in range(ROW_BLOCKS):
            for v in range(VIEWS):
                x_rows[(b, v)] = per_view.tile([P, IN_F], BF16, name="x_rows")

        def load_x(b, v):
            nc.sync.dma_start(out=x_rows[(b, v)][:], in_=views[v][b * P : (b + 1) * P, :])

        for cb in range(CLASS_BLOCKS):
            nc.sync.dma_start(out=cen_rows[:, cb, :], in_=centers[cb * P : (cb + 1) * P, :])
        nc.sync.dma_start(out=w_rows[0][:], in_=W_f)
        load_x(0, 0)
        nc.sync.dma_start(out=w_rows[1][:], in_=W_r)
        for v in range(1, VIEWS):
            load_x(0, v)
        for v in range(VIEWS):
            load_x(1, v)

        zeros = const.tile([P, P], F32)
        nc.vector.memset(zeros[:], 0.0)
        unread = psum.tile([P, P], F32, tag="bank")
        for step in range(HEAD_MATMULS):
            nc.tensor.matmul(out=unread[:], lhsT=zeros[:], rhs=zeros[:], start=True, stop=True)
        one = const.tile([P, 1], F32)
        nc.vector.memset(one[:], 1.0)
        one_root = const.tile([P, 1], F32)
        nc.scalar.activation(out=one_root[:], in_=one[:], func=ACT.Sqrt)
        ident_f32 = const.tile([P, P], F32)
        make_identity(nc, ident_f32[:])
        ident_bf = const.tile([P, P], BF16)
        nc.vector.tensor_copy(out=ident_bf[:], in_=ident_f32[:])

        w_codes = [const.tile([P, PASSES * FEAT], U32, align_bytes=64, name="w_codes%d" % w) for w in range(WEIGHTS)]
        w_scales = [const.tile([P, PASSES * FEAT], U8, align_bytes=64, name="w_scales%d" % w) for w in range(WEIGHTS)]
        x_codes, x_scales = {}, {}
        feat, feat_grouped, feat_codes, feat_scales, f2, dot, partial, root = {}, {}, {}, {}, {}, {}, {}, {}

        on_scalar, on_vector = nc.scalar.copy, nc.vector.tensor_copy

        waiting = [None]

        def quantise_waiting():
            if waiting[0] is not None:
                codes, scales, grouped = waiting[0]
                nc.vector.quantize_mx(out=codes[:].bitcast(FP8X4), scales=scales[:], in_=grouped[:])
            waiting[0] = None

        def quantise_later(codes, scales, grouped):
            quantise_waiting()
            waiting[0] = (codes, scales, grouped)

        def quantise_weight(w, copy_out):
            quantise_later(w_codes[w], w_scales[w], regroup_rows(nc, copy_out, psum, stage, w_rows[w], ident_f32, zeros if w == 1 else None))

        def quantise_view(b, v, copy_out):
            x_codes[(b, v)] = per_view.tile([P, PASSES * P], U32, align_bytes=64, name="x_codes")
            x_scales[(b, v)] = per_view.tile([P, PASSES * P], U8, align_bytes=64, name="x_scales")
            quantise_later(
                x_codes[(b, v)],
                x_scales[(b, v)],
                regroup_rows(nc, copy_out, psum, stage, x_rows[(b, v)], ident_f32, zeros if (b, v) in KEEP_BUSY else None),
            )

        feat_t = {}

        def project(b, views_of_bank):
            bank = psum.tile([FEAT, len(views_of_bank), P], F32, name="feat_t", tag="bank")
            for n, v in enumerate(views_of_bank):
                w = weight_of_view[v]
                for g in range(PASSES):
                    cols = slice(g * P, (g + 1) * P)
                    nc.tensor.matmul_mx(
                        out=bank[:, n, :],
                        lhsT=w_codes[w][:, cols].bitcast(FP8X4),
                        lhsT_scale=w_scales[w][:, cols],
                        rhs=x_codes[(b, v)][:, cols].bitcast(FP8X4),
                        rhs_scale=x_scales[(b, v)][:, cols],
                        start=(g == 0),
                        stop=(g == PASSES - 1),
                    )
            feat_t[(b, views_of_bank[0])] = bank

        def relu(b, views_of_bank, on_engine="scalar"):
            v0 = views_of_bank[0]
            bias_col = bias[weight_of_view[v0]][:, 0:1]
            feat_v = feat[b][:, v0 : v0 + len(views_of_bank), :]
            if on_engine == "vector":
                nc.vector.tensor_scalar(
                    out=feat_v, in0=feat_t[(b, v0)][:], scalar1=bias_col, scalar2=0.0, op0=ALU.add, op1=ALU.max
                )
            else:
                nc.scalar.activation(out=feat_v, in_=feat_t[(b, v0)][:], func=ACT.Relu, bias=bias_col)

        def round_features(b):
            feat_grouped[b] = per_block.tile([P, P, VIEWS], BF16, align_bytes=64, name="feat_grouped")
            nc.vector.tensor_copy(out=feat_grouped[b][:], in_=feat[b][:].rearrange("p v i -> p i v"))

        def quantise_features(b):
            feat_codes[b] = per_block.tile([P, P], U32, align_bytes=64, name="feat_codes")
            feat_scales[b] = per_block.tile([P, P], U8, align_bytes=64, name="feat_scales")
            nc.vector.quantize_mx(
                out=feat_codes[b][:].bitcast(FP8X4),
                scales=feat_scales[b][:],
                in_=feat_grouped[b][:].rearrange("p i v -> p (i v)"),
            )

        def sum_squared_features(b):
            feat_rows = psum.tile([P, VIEWS, FEAT], F32, tag="bank")
            for v in range(VIEWS):
                nc.tensor.transpose(feat_rows[:, v, :], feat[b][:, v, :], ident_f32[:])
            f2[b] = per_block.tile([P, 1], F32, name="f2")
            feat_squares = stage.tile([P, JOINED], F32)
            nc.scalar.activation(
                out=feat_squares[:], in_=feat_rows[:].rearrange("i v f -> i (v f)"), func=ACT.Square, accum_out=f2[b][:]
            )

        def multiply_by_centers(b):
            dot[b] = psum.tile([P, NCLASS], F32, name="dot", tag="bank")
            nc.tensor.matmul_mx(
                out=dot[b][:],
                lhsT=feat_codes[b][:].bitcast(FP8X4),
                lhsT_scale=feat_scales[b][:],
                rhs=cen_codes[:].bitcast(FP8X4),
                rhs_scale=cen_scales[:],
                start=True,
                stop=True,
            )

        def combine(b):
            partial[b] = per_block.tile([P, NCLASS], F32, name="partial")
            nc.vector.scalar_tensor_tensor(
                out=partial[b][:], in0=dot[b][:], scalar=-2.0, in1=c2_all[:], op0=ALU.mult, op1=ALU.add
            )

        def root_of(b):
            d2 = stage.tile([P, NCLASS], F32)
            nc.vector.tensor_scalar(
                out=d2[:], in0=partial[b][:], scalar1=f2[b][:, 0:1], scalar2=SQRT_FLOOR, op0=ALU.add, op1=ALU.max
            )
            root[b] = per_block.tile([P, NCLASS], F32, name="root")
            nc.scalar.activation(out=root[b][:], in_=d2[:], func=ACT.Sqrt)

        def store(b):
            score = stage.tile([P, NCLASS], F32)
            nc.vector.tensor_scalar_mul(out=score[:], in0=root[b][:], scalar1=-GAMMA)
            nc.sync.dma_start(out=out[b * P : (b + 1) * P, :], in_=score[:])

        cen_grouped = const.tile([P, NCLASS * PACK], BF16, align_bytes=64)
        for cb in range(CLASS_BLOCKS):
            cen_flipped = psum.tile([P, VIEWS, P], BF16, tag="bank")
            for v in range(VIEWS):
                nc.tensor.transpose(cen_flipped[:, v, :], cen_rows[:, cb, v * P : (v + 1) * P], ident_bf[:])
            nc.vector.tensor_copy(
                out=cen_grouped[:, cb * P * PACK : (cb + 1) * P * PACK].rearrange("p (c v) -> p c v", v=VIEWS),
                in_=cen_flipped[:].rearrange("p v c -> p c v"),
            )
        cen_codes = const.tile([P, NCLASS], U32, align_bytes=64)
        cen_scales = const.tile([P, NCLASS], U8, align_bytes=64)
        quantise_later(cen_codes, cen_scales, cen_grouped)

        c2_col = const.tile([P, CLASS_BLOCKS], F32)
        cen_squares = const.tile([P, CLASS_BLOCKS, JOINED], F32)
        for cb in range(CLASS_BLOCKS):
            nc.scalar.activation(
                out=cen_squares[:, cb, :], in_=cen_rows[:, cb, :], func=ACT.Square, accum_out=c2_col[:, cb : cb + 1]
            )

        quantise_weight(0, on_scalar)
        quantise_view(0, 0, on_vector)
        quantise_weight(1, on_scalar)
        c2_spread = psum.tile([P, NCLASS], F32, tag="bank")
        for cb in range(CLASS_BLOCKS):
            nc.tensor.transpose(
                c2_spread[:, cb * P : (cb + 1) * P], c2_col[:, cb : cb + 1].to_broadcast([P, P]), ident_f32[:]
            )
        quantise_view(0, 1, on_scalar)
        c2_all = const.tile([P, NCLASS], F32)
        nc.vector.tensor_copy(out=c2_all[:], in_=c2_spread[:])
        quantise_view(0, 2, on_scalar)
        quantise_view(0, 3, on_vector)
        for v in range(VIEWS):
            quantise_view(1, v, on_scalar)
        for b in range(ROW_BLOCKS):
            feat[b] = per_block.tile([FEAT, VIEWS, P], F32, name="feat")
        project(0, [0])
        project(0, [1, 2, 3])
        relu(0, [0])
        relu(0, [1, 2, 3])
        quantise_waiting()
        for v in range(VIEWS):
            project(1, [v])
            relu(1, [v], "vector" if v < 2 else "scalar")
        for b in range(ROW_BLOCKS):
            round_features(b)
        for b in range(ROW_BLOCKS):
            quantise_features(b)
        for b in range(ROW_BLOCKS):
            sum_squared_features(b)
        for b in range(ROW_BLOCKS):
            multiply_by_centers(b)
        for b in range(ROW_BLOCKS):
            combine(b)
        for b in range(ROW_BLOCKS):
            root_of(b)
        for b in range(ROW_BLOCKS):
            store(b)
